import numpy as np
import ml_dtypes


def mxq(x, axis, fmt="e4m3"):
    dtype, down = {"e4m3": (ml_dtypes.float8_e4m3fn, 7), "e5m2": (ml_dtypes.float8_e5m2, 14)}[fmt]
    v = np.moveaxis(np.asarray(x, np.float32).astype(ml_dtypes.bfloat16).astype(np.float64), axis, -1)
    blocks = v.reshape(v.shape[:-1] + (-1, 32))
    amax = np.abs(blocks).max(-1, keepdims=True)
    byte = np.maximum(np.where(amax > 0, np.frexp(amax)[1] - 1 + 127, 0) - down, 1)
    scale = np.exp2(byte - 127.0)
    codes = (blocks / scale).astype(np.float32).astype(dtype).astype(np.float64)
    return np.moveaxis((codes * scale).reshape(v.shape), -1, axis)


WIDE = False


def mx_kscale(k):
    if not WIDE:
        return np.ones(k)
    levels = np.array([10, -10, 5, -5, 0])
    if k % 512:
        return np.exp2(np.random.permutation(np.resize(levels, k // 32))).repeat(32)
    a = np.empty((k // 512, 16))
    for p in range(k // 512):
        a[p, :8] = np.random.permutation(np.resize(levels, 8))
        for g in range(8):
            far = levels[np.abs(levels - a[p, g]) >= 10]
            a[p, g + 8] = far[np.random.randint(len(far))]
    return np.exp2(a.ravel()).repeat(32)


BF16 = ml_dtypes.bfloat16


def bf(x):
    return np.asarray(x, np.float32).astype(BF16)


def f64(x):
    return np.asarray(x).astype(np.float64)


B, T, E = 2, 1024, 512


def setup_inputs():
    s, t = mx_kscale(E), mx_kscale(E)
    r = np.random.standard_normal
    return {"x1": bf(r((B, T, E)) * s), "x2": bf(r((B, T, E)) * s),
            "W1": bf(r((E, E)) * 0.4 / np.sqrt(E) / s[:, None] * t), "W2": bf(r((E, E)) * 0.4 / np.sqrt(E) / s[:, None] / t),
            "b1": bf(r((T, E)) * 0.1 * t), "b2": bf(r((T, E)) * 0.1 / t)}


def reference(x1, x2, W1, W2, b1, b2):
    e1t = np.maximum((mxq(f64(x1), 2, "e4m3") @ mxq(f64(W1), 0, "e4m3")) + f64(b1), 0.0)
    e2t = np.maximum((mxq(f64(x2), 2, "e4m3") @ mxq(f64(W2), 0, "e4m3")) + f64(b2), 0.0)
    scores = mxq(e2t, 2, "e4m3") @ mxq(e1t, 2, "e4m3").transpose(0, 2, 1)
    ex = np.exp(scores - scores.max(-1, keepdims=True))
    return ex / ex.sum(-1, keepdims=True)

@@ -1,0 +1,345 @@
+from contextlib import ExitStack
+
+import concourse.mybir as mybir
+from concourse.masks import make_identity
+
+F32 = mybir.dt.float32
+BF16 = mybir.dt.bfloat16
+U32 = mybir.dt.uint32
+U8 = mybir.dt.uint8
+FP8X4 = mybir.dt.float8_e4m3fn_x4
+ALU = mybir.AluOpType
+ACT = mybir.ActivationFunctionType
+AX = mybir.AxisListType
+
+B, T, E = 2, 1024, 512
+P = 128
+BANK = 512
+SLAB = 256
+N_SLABS = 2 * B * T // SLAB
+N_ROW_TILES = B * T // P
+FLOPS = 2 * (2 * B * T * E * E) + 2 * B * T * T * E
+
+SCALAR_RELU_FROM = 5
+VECTOR_SCALES_FROM = 12
+
+
+def tile_attentionmm_pa_kernel(tc, x1, x2, W1, W2, b1, b2, out):
+    nc = tc.nc
+    with ExitStack() as ctx:
+        ctx.enter_context(tc.manual_schedule())
+        keep = ctx.enter_context(tc.tile_pool(name="keep", bufs=1))
+        work = ctx.enter_context(tc.tile_pool(name="work", bufs=5))
+        expool = ctx.enter_context(tc.tile_pool(name="expool", bufs=8))
+        small = ctx.enter_context(tc.tile_pool(name="small", bufs=8))
+        psum = ctx.enter_context(tc.psum_pool(name="psum", bufs=2))
+
+        ws = {1: W1, 2: W2}
+        x_view = {
+            1: x1.rearrange("b (n p) k -> p b n k", p=P),
+            2: x2.rearrange("b (p n) k -> p b n k", p=P),
+        }
+        b_view = {
+            1: b1.rearrange("(n p) f -> p n f", p=P),
+            2: b2.rearrange("(p n) f -> p n f", p=P),
+        }
+        out_view = out.rearrange("b (p n) j -> p b n j", p=P)
+
+        x_sb, b_sb, w_sb, wg, w_codes, w_scales = {}, {}, {}, {}, {}, {}
+        x_codes, x_scales, bT, e_codes, e_scales = {}, {}, {}, {}, {}
+        for s in (1, 2):
+            x_sb[s] = keep.tile([P, B, 8, E], BF16, name="x_sb%d" % s)
+            b_sb[s] = keep.tile([P, 8, E], BF16, name="b_sb%d" % s)
+            w_sb[s] = keep.tile([P, 4, E], BF16, name="w_sb%d" % s)
+            wg[s] = keep.tile([P, E, 4], BF16, name="wg%d" % s, align_bytes=64)
+            w_codes[s] = keep.tile([P, E], U32, name="w_codes%d" % s, align_bytes=64)
+            w_scales[s] = keep.tile([P, E], U8, name="w_scales%d" % s, align_bytes=64)
+            x_codes[s] = keep.tile([P, B * T], U32, name="x_codes%d" % s, align_bytes=64)
+            x_scales[s] = keep.tile([P, B * T], U8, name="x_scales%d" % s, align_bytes=64)
+            bT[s] = keep.tile([P, T, 4], BF16, name="bT%d" % s, align_bytes=64)
+            e_codes[s] = keep.tile([P, B * T], U32, name="e_codes%d" % s, align_bytes=64)
+            e_scales[s] = keep.tile([P, B * T], U8, name="e_scales%d" % s, align_bytes=64)
+
+        def load_w(s):
+            nc.sync.dma_start(out=w_sb[s][:], in_=ws[s].rearrange("(q j) c -> q j c", j=4))
+
+        def load_x(s, b, n0, n1):
+            nc.sync.dma_start(out=x_sb[s][:, b, n0:n1, :], in_=x_view[s][:, b, n0:n1, :])
+
+        def load_b(s, n0, n1):
+            nc.sync.dma_start(out=b_sb[s][:, n0:n1, :], in_=b_view[s][:, n0:n1, :])
+
+        load_w(1)
+        for q in range(4):
+            load_x(1, 0, 2 * q, 2 * q + 2)
+            load_b(1, 2 * q, 2 * q + 2)
+        load_w(2)
+        for half in range(2):
+            load_x(2, 0, 4 * half, 4 * half + 4)
+            load_b(2, 4 * half, 4 * half + 4)
+        load_x(1, 1, 0, 8)
+        load_x(2, 1, 0, 8)
+
+        ident = keep.tile([P, P], F32, name="ident")
+        make_identity(nc, ident[:])
+        warm = keep.tile([P, 1], F32, name="warm")
+        nc.vector.memset(warm[:], 0.0)
+        nc.scalar.activation(out=warm[:], in_=warm[:], func=ACT.Exp)
+
+        slabs = [(s, b, q) for b in range(B) for s in (1, 2) for q in range(4)]
+        xg, pre, s1, sc, part, negm, ex, sums, tot, rs = {}, {}, {}, {}, {}, {}, {}, {}, {}, {}
+
+        def regroup_w(s, u, copy):
+            copy(
+                out=wg[s][:, 256 * u : 256 * u + 256, :].rearrange("q (t p) j -> q t p j", t=2),
+                in_=w_sb[s][:].rearrange("q j (p t) -> q t p j", t=4)[:, 2 * u : 2 * u + 2, :, :],
+            )
+
+        def quantise_w(s):
+            nc.vector.quantize_mx(
+                out=w_codes[s][:].bitcast(FP8X4),
+                scales=w_scales[s][:],
+                in_=wg[s][:].rearrange("q f s -> q (f s)"),
+            )
+
+        def transpose_pair(src, dst):
+            bank = psum.tile([P, BANK], F32, name="tp", tag="tp")
+            planes = bank[:].rearrange("p (a u t) -> p a u t", a=2, u=2)
+            for a in range(2):
+                words = src[:, a, :].bitcast(F32)
+                for u in range(2):
+                    nc.tensor.transpose(planes[:, a, u, :], words[:, u : 256 : 2], ident[:])
+            nc.scalar.copy(
+                out=dst.rearrange("p t j -> p (t j)").bitcast(F32).rearrange("p (a t u) -> p a t u", a=2, u=2),
+                in_=planes.rearrange("p a u t -> p a t u"),
+            )
+
+        def transpose_slab(h):
+            s, b, q = slabs[h]
+            xg[h] = work.tile([P, SLAB, 4], BF16, name="xg", tag="xg", align_bytes=64)
+            transpose_pair(x_sb[s][:, b, 2 * q : 2 * q + 2, :], xg[h][:])
+            if b == 0:
+                transpose_pair(b_sb[s][:, 2 * q : 2 * q + 2, :], bT[s][:, SLAB * q : SLAB * q + SLAB, :])
+
+        def first_column(h):
+            s, b, q = slabs[h]
+            return b * T + q * SLAB
+
+        def quantise_x(h):
+            if h >= N_SLABS:
+                return
+            s = slabs[h][0]
+            c0 = first_column(h)
+            nc.vector.quantize_mx(
+                out=x_codes[s][:, c0 : c0 + SLAB].bitcast(FP8X4),
+                scales=x_scales[s][:, c0 : c0 + SLAB],
+                in_=xg[h][:].rearrange("p t j -> p (t j)"),
+            )
+
+        def project(h, a):
+            if h >= N_SLABS:
+                return
+            s = slabs[h][0]
+            c0 = first_column(h) + P * a
+            s1[h, a] = psum.tile([P, BANK], F32, name="s1", tag="s1")
+            by_j = s1[h, a][:].rearrange("p (j t) -> p j t", j=4)
+            for j in range(4):
+                nc.tensor.matmul_mx(
+                    out=by_j[:, j, :],
+                    lhsT=w_codes[s][:, P * j : P * j + P].bitcast(FP8X4),
+                    lhsT_scale=w_scales[s][:, P * j : P * j + P],
+                    rhs=x_codes[s][:, c0 : c0 + P].bitcast(FP8X4),
+                    rhs_scale=x_scales[s][:, c0 : c0 + P],
+                    start=True,
+                    stop=True,
+                )
+
+        def add_bias(h, a):
+            s, b, q = slabs[h]
+            if a == 0:
+                pre[h] = work.tile([P, SLAB, 4], BF16, name="pre", tag="pre", align_bytes=64)
+            nc.vector.tensor_tensor(
+                out=pre[h][:, P * a : P * a + P, :],
+                in0=s1[h, a][:].rearrange("p (j t) -> p t j", j=4),
+                in1=bT[s][:, SLAB * q + P * a : SLAB * q + P * a + P, :],
+                op=ALU.add,
+            )
+
+        def relu(h):
+            flat = pre[h][:].rearrange("p t j -> p (t j)")
+            if h >= SCALAR_RELU_FROM:
+                nc.scalar.activation(out=flat, in_=flat, func=ACT.Relu)
+            else:
+                nc.vector.tensor_scalar_max(out=flat, in0=flat, scalar1=0.0)
+
+        def quantise_e(h):
+            if h < 0:
+                return
+            s = slabs[h][0]
+            c0 = first_column(h)
+            nc.vector.quantize_mx(
+                out=e_codes[s][:, c0 : c0 + SLAB].bitcast(FP8X4),
+                scales=e_scales[s][:, c0 : c0 + SLAB],
+                in_=pre[h][:].rearrange("p t j -> p (t j)"),
+            )
+
+        def scores(t):
+            tag = {N_ROW_TILES - 2: "tp", N_ROW_TILES - 1: "s1"}.get(t, "sc")
+            for hh in range(2):
+                sc[t, hh] = psum.tile([P, BANK], F32, name="sc", tag=tag, bufs=4 if tag == "sc" else 2)
+                j0 = (t // 8) * T + BANK * hh
+                nc.tensor.matmul_mx(
+                    out=sc[t, hh][:],
+                    lhsT=e_codes[2][:, P * t : P * t + P].bitcast(FP8X4),
+                    lhsT_scale=e_scales[2][:, P * t : P * t + P],
+                    rhs=e_codes[1][:, j0 : j0 + BANK].bitcast(FP8X4),
+                    rhs_scale=e_scales[1][:, j0 : j0 + BANK],
+                    start=True,
+                    stop=True,
+                )
+
+        def bank_max(t, hh):
+            if hh == 0:
+                part[t] = small.tile([P, 2], F32, name="part", tag="part")
+            nc.vector.tensor_reduce(out=part[t][:, hh : hh + 1], in_=sc[t, hh][:], axis=AX.X, op=ALU.max)
+
+        def row_max(t):
+            negm[t] = small.tile([P, 1], F32, name="negm", tag="negm")
+            nc.vector.tensor_reduce(out=negm[t][:], in_=part[t][:], axis=AX.X, op=ALU.max, negate=True)
+
+        def exponent(t):
+            ex[t] = expool.tile([P, T], F32, name="ex", tag="ex")
+            sums[t] = small.tile([P, 2], F32, name="sums", tag="sums")
+            for hh in range(2):
+                nc.scalar.activation(
+                    out=ex[t][:, BANK * hh : BANK * hh + BANK],
+                    in_=sc[t, hh][:],
+                    func=ACT.Exp,
+                    bias=negm[t][:, 0:1],
+                    scale=1.0,
+                    accum_out=sums[t][:, hh : hh + 1],
+                )
+
+        def row_sum(t):
+            tot[t] = small.tile([P, 1], F32, name="tot", tag="tot")
+            nc.vector.tensor_reduce(out=tot[t][:], in_=sums[t][:], axis=AX.X, op=ALU.add)
+
+        def inverse(t):
+            rs[t] = small.tile([P, 1], F32, name="rs", tag="rs")
+            nc.vector.reciprocal(out=rs[t][:], in_=tot[t][:])
+
+        def scale_and_store(t):
+            if t >= VECTOR_SCALES_FROM:
+                nc.vector.tensor_scalar_mul(out=ex[t][:], in0=ex[t][:], scalar1=rs[t][:, 0:1])
+            else:
+                nc.gpsimd.tensor_scalar(
+                    out=ex[t][:], in0=ex[t][:], scalar1=rs[t][:, 0:1], scalar2=0.0, op0=ALU.mult, op1=ALU.add
+                )
+            nc.sync.dma_start(out=out_view[:, t // 8, t % 8, :], in_=ex[t][:])
+
+        def row_tiles_of(c):
+            if c < 6:
+                return []
+            if c < 14:
+                return [c - 6]
+            return [2 * c - 20, 2 * c - 19]
+
+        def last_slab_of(t):
+            return 8 * (t // 8) + 4 + (t % 8) // 2
+
+        regroup_w(1, 0, nc.vector.tensor_copy)
+        regroup_w(1, 1, nc.vector.tensor_copy)
+        quantise_w(1)
+        transpose_slab(0)
+        transpose_slab(1)
+        quantise_x(0)
+        project(0, 0)
+        project(0, 1)
+        transpose_slab(2)
+        transposed = 3
+
+        for c in range(N_SLABS):
+            tiles = row_tiles_of(c)
+            two = len(tiles) == 2
+            done = [t for t in range(tiles[0] - 1, tiles[-1]) if t >= 0] if tiles else []
+            fresh = bool(tiles) and last_slab_of(tiles[0]) == c - 2
+
+            add_bias(c, 0)
+            if c == 0:
+                quantise_x(1)
+            project(c + 1, 0)
+            if tiles and not fresh:
+                bank_max(tiles[0], 0)
+            add_bias(c, 1)
+            project(c + 1, 1)
+            if fresh:
+                bank_max(tiles[0], 0)
+            if c >= SCALAR_RELU_FROM:
+                relu(c)
+            if tiles:
+                bank_max(tiles[0], 1)
+            if two:
+                bank_max(tiles[1], 0)
+
+            quantise_x(c + 2)
+            if c < SCALAR_RELU_FROM:
+                relu(c)
+            if tiles:
+                row_max(tiles[0])
+                exponent(tiles[0])
+            if two:
+                bank_max(tiles[1], 1)
+            if done:
+                row_sum(done[0])
+            quantise_e(c - 1)
+            if two:
+                row_max(tiles[1])
+                exponent(tiles[1])
+                row_sum(done[1])
+            if c == 1:
+                regroup_w(2, 1, nc.vector.tensor_copy)
+            if c == 2:
+                quantise_w(2)
+            if c == N_SLABS - 1:
+                quantise_e(c)
+            for t in done:
+                inverse(t)
+            for t in done:
+                scale_and_store(t)
+            if c == 1:
+                regroup_w(2, 0, nc.scalar.copy)
+
+            ahead = 3 if c < 5 else 4
+            while transposed < min(N_SLABS, c + ahead + 1):
+                transpose_slab(transposed)
+                transposed += 1
+            for t in row_tiles_of(c + 1):
+                scores(t)
+
+        scores(14)
+        scores(15)
+        bank_max(12, 0)
+        bank_max(12, 1)
+        row_sum(11)
+        row_max(12)
+        exponent(12)
+        inverse(11)
+        scale_and_store(11)
+        bank_max(13, 0)
+        bank_max(13, 1)
+        for t in (14, 15):
+            bank_max(t, 0)
+            row_max(t - 1)
+            exponent(t - 1)
+            bank_max(t, 1)
+            row_sum(t - 2)
+        row_max(15)
+        exponent(15)
+        for t in (12, 13):
+            inverse(t)
+        for t in (12, 13):
+            scale_and_store(t)
+        for t in (14, 15):
+            row_sum(t)
+            inverse(t)
+            scale_and_store(t)

@@ -20,8 +20,10 @@ N_SLABS = 2 * B * T // SLAB
 N_ROW_TILES = B * T // P
 FLOPS = 2 * (2 * B * T * E * E) + 2 * B * T * T * E
 
-SCALAR_RELU_FROM = 5
+W1_SPLIT = 320
+W2_SPLIT = 320
 VECTOR_SCALES_FROM = 12
+AHEAD = 3
 
 
 def tile_attentionmm_pa_kernel(tc, x1, x2, W1, W2, b1, b2, out):
@@ -29,56 +31,58 @@ def tile_attentionmm_pa_kernel(tc, x1, x2, W1, W2, b1, b2, out):
     with ExitStack() as ctx:
         ctx.enter_context(tc.manual_schedule())
         keep = ctx.enter_context(tc.tile_pool(name="keep", bufs=1))
-        work = ctx.enter_context(tc.tile_pool(name="work", bufs=5))
+        work = ctx.enter_context(tc.tile_pool(name="work", bufs=6))
         expool = ctx.enter_context(tc.tile_pool(name="expool", bufs=8))
         small = ctx.enter_context(tc.tile_pool(name="small", bufs=8))
         psum = ctx.enter_context(tc.psum_pool(name="psum", bufs=2))
 
         ws = {1: W1, 2: W2}
         x_view = {
-            1: x1.rearrange("b (n p) k -> p b n k", p=P),
-            2: x2.rearrange("b (p n) k -> p b n k", p=P),
+            1: x1.rearrange("b (q p a) k -> p b q a k", q=4, a=2),
+            2: x2.rearrange("b (p q a) k -> p b q a k", q=4, a=2),
         }
         b_view = {
-            1: b1.rearrange("(n p) f -> p n f", p=P),
-            2: b2.rearrange("(p n) f -> p n f", p=P),
+            1: b1.rearrange("(q p a) f -> p q a f", q=4, a=2),
+            2: b2.rearrange("(p q a) f -> p q a f", q=4, a=2),
         }
         out_view = out.rearrange("b (p n) j -> p b n j", p=P)
 
         x_sb, b_sb, w_sb, wg, w_codes, w_scales = {}, {}, {}, {}, {}, {}
-        x_codes, x_scales, bT, e_codes, e_scales = {}, {}, {}, {}, {}
+        x_codes, x_scales, e_codes, e_scales = {}, {}, {}, {}
         for s in (1, 2):
-            x_sb[s] = keep.tile([P, B, 8, E], BF16, name="x_sb%d" % s)
-            b_sb[s] = keep.tile([P, 8, E], BF16, name="b_sb%d" % s)
+            x_sb[s] = keep.tile([P, B, 4, 2, E], BF16, name="x_sb%d" % s)
+            b_sb[s] = keep.tile([P, 4, 2, E], BF16, name="b_sb%d" % s)
             w_sb[s] = keep.tile([P, 4, E], BF16, name="w_sb%d" % s)
             wg[s] = keep.tile([P, E, 4], BF16, name="wg%d" % s, align_bytes=64)
             w_codes[s] = keep.tile([P, E], U32, name="w_codes%d" % s, align_bytes=64)
             w_scales[s] = keep.tile([P, E], U8, name="w_scales%d" % s, align_bytes=64)
             x_codes[s] = keep.tile([P, B * T], U32, name="x_codes%d" % s, align_bytes=64)
             x_scales[s] = keep.tile([P, B * T], U8, name="x_scales%d" % s, align_bytes=64)
-            bT[s] = keep.tile([P, T, 4], BF16, name="bT%d" % s, align_bytes=64)
             e_codes[s] = keep.tile([P, B * T], U32, name="e_codes%d" % s, align_bytes=64)
             e_scales[s] = keep.tile([P, B * T], U8, name="e_scales%d" % s, align_bytes=64)
 
         def load_w(s):
             nc.sync.dma_start(out=w_sb[s][:], in_=ws[s].rearrange("(q j) c -> q j c", j=4))
 
-        def load_x(s, b, n0, n1):
-            nc.sync.dma_start(out=x_sb[s][:, b, n0:n1, :], in_=x_view[s][:, b, n0:n1, :])
+        def load_x(s, b, q0, q1):
+            nc.sync.dma_start(out=x_sb[s][:, b, q0:q1, :, :], in_=x_view[s][:, b, q0:q1, :, :])
 
-        def load_b(s, n0, n1):
-            nc.sync.dma_start(out=b_sb[s][:, n0:n1, :], in_=b_view[s][:, n0:n1, :])
+        def load_b(s, q0, q1):
+            nc.sync.dma_start(out=b_sb[s][:, q0:q1, :, :], in_=b_view[s][:, q0:q1, :, :])
 
+        load_x(1, 0, 0, 1)
         load_w(1)
-        for q in range(4):
-            load_x(1, 0, 2 * q, 2 * q + 2)
-            load_b(1, 2 * q, 2 * q + 2)
+        load_x(1, 0, 1, 2)
+        load_b(1, 0, 1)
         load_w(2)
+        load_x(1, 0, 2, 3)
+        load_x(1, 0, 3, 4)
+        load_b(1, 1, 4)
         for half in range(2):
-            load_x(2, 0, 4 * half, 4 * half + 4)
-            load_b(2, 4 * half, 4 * half + 4)
-        load_x(1, 1, 0, 8)
-        load_x(2, 1, 0, 8)
+            load_x(2, 0, 2 * half, 2 * half + 2)
+            load_b(2, 2 * half, 2 * half + 2)
+        load_x(1, 1, 0, 4)
+        load_x(2, 1, 0, 4)
 
         ident = keep.tile([P, P], F32, name="ident")
         make_identity(nc, ident[:])
@@ -87,43 +91,35 @@ def tile_attentionmm_pa_kernel(tc, x1, x2, W1, W2, b1, b2, out):
         nc.scalar.activation(out=warm[:], in_=warm[:], func=ACT.Exp)
 
         slabs = [(s, b, q) for b in range(B) for s in (1, 2) for q in range(4)]
-        xg, pre, s1, sc, part, negm, ex, sums, tot, rs = {}, {}, {}, {}, {}, {}, {}, {}, {}, {}
+        xg, pre, eg, s1, sc, part, negm, ex, sums, tot, rs = {}, {}, {}, {}, {}, {}, {}, {}, {}, {}, {}
 
-        def regroup_w(s, u, copy):
-            copy(
-                out=wg[s][:, 256 * u : 256 * u + 256, :].rearrange("q (t p) j -> q t p j", t=2),
-                in_=w_sb[s][:].rearrange("q j (p t) -> q t p j", t=4)[:, 2 * u : 2 * u + 2, :, :],
-            )
+        def regroup_w(s, c0, c1, copy):
+            copy(out=wg[s][:, c0:c1, :], in_=w_sb[s][:, :, c0:c1].rearrange("q j c -> q c j"))
 
         def quantise_w(s):
             nc.vector.quantize_mx(
                 out=w_codes[s][:].bitcast(FP8X4),
                 scales=w_scales[s][:],
-                in_=wg[s][:].rearrange("q f s -> q (f s)"),
+                in_=wg[s][:].rearrange("q f j -> q (f j)"),
             )
-
-        def transpose_pair(src, dst):
-            bank = psum.tile([P, BANK], F32, name="tp", tag="tp")
-            planes = bank[:].rearrange("p (a u t) -> p a u t", a=2, u=2)
-            for a in range(2):
-                words = src[:, a, :].bitcast(F32)
-                for u in range(2):
-                    nc.tensor.transpose(planes[:, a, u, :], words[:, u : 256 : 2], ident[:])
-            nc.scalar.copy(
-                out=dst.rearrange("p t j -> p (t j)").bitcast(F32).rearrange("p (a t u) -> p a t u", a=2, u=2),
-                in_=planes.rearrange("p a u t -> p a t u"),
-            )
-
-        def transpose_slab(h):
-            s, b, q = slabs[h]
-            xg[h] = work.tile([P, SLAB, 4], BF16, name="xg", tag="xg", align_bytes=64)
-            transpose_pair(x_sb[s][:, b, 2 * q : 2 * q + 2, :], xg[h][:])
-            if b == 0:
-                transpose_pair(b_sb[s][:, 2 * q : 2 * q + 2, :], bT[s][:, SLAB * q : SLAB * q + SLAB, :])
 
         def first_column(h):
             s, b, q = slabs[h]
             return b * T + q * SLAB
+
+        def transpose_x(h):
+            s, b, q = slabs[h]
+            xg[h] = work.tile([P, SLAB, 4], BF16, name="xg", tag="xg", align_bytes=64)
+            bank = psum.tile([P, BANK], F32, name="tx", tag="tx", bufs=1)
+            planes = bank[:].rearrange("p (u a t) -> p u a t", u=2, a=2)
+            for a in range(2):
+                words = x_sb[s][:, b, q, a, :].bitcast(F32)
+                for u in range(2):
+                    nc.tensor.transpose(planes[:, u, a, :], words[:, u : 256 : 2], ident[:])
+            nc.scalar.copy(
+                out=xg[h][:].rearrange("p m j -> p (m j)").bitcast(F32).rearrange("p (m u) -> p m u", u=2),
+                in_=bank[:].rearrange("p (u m) -> p m u", u=2),
+            )
 
         def quantise_x(h):
             if h >= N_SLABS:
@@ -133,7 +129,7 @@ def tile_attentionmm_pa_kernel(tc, x1, x2, W1, W2, b1, b2, out):
             nc.vector.quantize_mx(
                 out=x_codes[s][:, c0 : c0 + SLAB].bitcast(FP8X4),
                 scales=x_scales[s][:, c0 : c0 + SLAB],
-                in_=xg[h][:].rearrange("p t j -> p (t j)"),
+                in_=xg[h][:].rearrange("p m j -> p (m j)"),
             )
 
         def project(h, a):
@@ -142,35 +138,44 @@ def tile_attentionmm_pa_kernel(tc, x1, x2, W1, W2, b1, b2, out):
             s = slabs[h][0]
             c0 = first_column(h) + P * a
             s1[h, a] = psum.tile([P, BANK], F32, name="s1", tag="s1")
-            by_j = s1[h, a][:].rearrange("p (j t) -> p j t", j=4)
-            for j in range(4):
-                nc.tensor.matmul_mx(
-                    out=by_j[:, j, :],
-                    lhsT=w_codes[s][:, P * j : P * j + P].bitcast(FP8X4),
-                    lhsT_scale=w_scales[s][:, P * j : P * j + P],
-                    rhs=x_codes[s][:, c0 : c0 + P].bitcast(FP8X4),
-                    rhs_scale=x_scales[s][:, c0 : c0 + P],
-                    start=True,
-                    stop=True,
-                )
+            nc.tensor.matmul_mx(
+                out=s1[h, a][:],
+                lhsT=x_codes[s][:, c0 : c0 + P].bitcast(FP8X4),
+                lhsT_scale=x_scales[s][:, c0 : c0 + P],
+                rhs=w_codes[s][:].bitcast(FP8X4),
+                rhs_scale=w_scales[s][:],
+                start=True,
+                stop=True,
+            )
 
         def add_bias(h, a):
             s, b, q = slabs[h]
             if a == 0:
-                pre[h] = work.tile([P, SLAB, 4], BF16, name="pre", tag="pre", align_bytes=64)
+                pre[h] = work.tile([P, 2, E], BF16, name="pre", tag="pre", align_bytes=64)
             nc.vector.tensor_tensor(
-                out=pre[h][:, P * a : P * a + P, :],
-                in0=s1[h, a][:].rearrange("p (j t) -> p t j", j=4),
-                in1=bT[s][:, SLAB * q + P * a : SLAB * q + P * a + P, :],
+                out=pre[h][:, a, :].rearrange("q (u p e) -> q u p e", u=2, e=2),
+                in0=s1[h, a][:].rearrange("q (p u e) -> q u p e", u=2, e=2),
+                in1=b_sb[s][:, q, a, :].rearrange("q (p u e) -> q u p e", u=2, e=2),
                 op=ALU.add,
             )
 
-        def relu(h):
-            flat = pre[h][:].rearrange("p t j -> p (t j)")
-            if h >= SCALAR_RELU_FROM:
-                nc.scalar.activation(out=flat, in_=flat, func=ACT.Relu)
+        def transpose_e(h):
+            s = slabs[h][0]
+            eg[h] = work.tile([P, SLAB, 4], BF16, name="eg", tag="eg", align_bytes=64)
+            bank = psum.tile([P, BANK], F32, name="te", tag="te", bufs=1)
+            if s == 1:
+                planes = bank[:].rearrange("p (a u t) -> p u a t", u=2, a=2)
+                src = bank[:].bitcast(BF16).rearrange("p (k t e) -> p t k e", k=4, e=2)
+                dst = eg[h][:].rearrange("p (t a) (u e) -> p t (a u) e", a=2, e=2)
             else:
-                nc.vector.tensor_scalar_max(out=flat, in0=flat, scalar1=0.0)
+                planes = bank[:].rearrange("p (u a t) -> p u a t", u=2, a=2)
+                src = bank[:].bitcast(BF16).rearrange("p (u m e) -> p m u e", u=2, e=2)
+                dst = eg[h][:].rearrange("p m (u e) -> p m u e", e=2)
+            for a in range(2):
+                words = pre[h][:, a, :].bitcast(F32)
+                for u in range(2):
+                    nc.tensor.transpose(planes[:, u, a, :], words[:, P * u : P * u + P], ident[:])
+            nc.scalar.activation(out=dst, in_=src, func=ACT.Relu)
 
         def quantise_e(h):
             if h < 0:
@@ -180,13 +185,18 @@ def tile_attentionmm_pa_kernel(tc, x1, x2, W1, W2, b1, b2, out):
             nc.vector.quantize_mx(
                 out=e_codes[s][:, c0 : c0 + SLAB].bitcast(FP8X4),
                 scales=e_scales[s][:, c0 : c0 + SLAB],
-                in_=pre[h][:].rearrange("p t j -> p (t j)"),
+                in_=eg[h][:].rearrange("p m j -> p (m j)"),
             )
 
         def scores(t):
-            tag = {N_ROW_TILES - 2: "tp", N_ROW_TILES - 1: "s1"}.get(t, "sc")
             for hh in range(2):
-                sc[t, hh] = psum.tile([P, BANK], F32, name="sc", tag=tag, bufs=4 if tag == "sc" else 2)
+                if t == N_ROW_TILES - 4:
+                    tag, n = "s1", 2
+                elif t == N_ROW_TILES - 3:
+                    tag, n = ("tx", "te")[hh], 1
+                else:
+                    tag, n = "sc", 4
+                sc[t, hh] = psum.tile([P, BANK], F32, name="sc", tag=tag, bufs=n)
                 j0 = (t // 8) * T + BANK * hh
                 nc.tensor.matmul_mx(
                     out=sc[t, hh][:],
@@ -244,102 +254,111 @@ def tile_attentionmm_pa_kernel(tc, x1, x2, W1, W2, b1, b2, out):
                 return [c - 6]
             return [2 * c - 20, 2 * c - 19]
 
-        def last_slab_of(t):
-            return 8 * (t // 8) + 4 + (t % 8) // 2
-
-        regroup_w(1, 0, nc.vector.tensor_copy)
-        regroup_w(1, 1, nc.vector.tensor_copy)
-        quantise_w(1)
-        transpose_slab(0)
-        transpose_slab(1)
+        transpose_x(0)
+        regroup_w(1, 0, W1_SPLIT, nc.vector.tensor_copy)
+        regroup_w(1, W1_SPLIT, E, nc.scalar.copy)
         quantise_x(0)
+        quantise_w(1)
+        transpose_x(1)
         project(0, 0)
         project(0, 1)
-        transpose_slab(2)
+        regroup_w(2, 0, W2_SPLIT, nc.vector.tensor_copy)
+        regroup_w(2, W2_SPLIT, E, nc.scalar.copy)
+        transpose_x(2)
         transposed = 3
 
         for c in range(N_SLABS):
             tiles = row_tiles_of(c)
-            two = len(tiles) == 2
-            done = [t for t in range(tiles[0] - 1, tiles[-1]) if t >= 0] if tiles else []
-            fresh = bool(tiles) and last_slab_of(tiles[0]) == c - 2
-
+            if c >= 1:
+                while transposed < min(N_SLABS, c + AHEAD + 1):
+                    transpose_x(transposed)
+                    transposed += 1
             add_bias(c, 0)
             if c == 0:
                 quantise_x(1)
+            if c <= 5:
+                quantise_e(c - 2)
             project(c + 1, 0)
-            if tiles and not fresh:
-                bank_max(tiles[0], 0)
             add_bias(c, 1)
             project(c + 1, 1)
-            if fresh:
-                bank_max(tiles[0], 0)
-            if c >= SCALAR_RELU_FROM:
-                relu(c)
-            if tiles:
-                bank_max(tiles[0], 1)
-            if two:
-                bank_max(tiles[1], 0)
-
-            quantise_x(c + 2)
-            if c < SCALAR_RELU_FROM:
-                relu(c)
-            if tiles:
-                row_max(tiles[0])
-                exponent(tiles[0])
-            if two:
-                bank_max(tiles[1], 1)
-            if done:
-                row_sum(done[0])
-            quantise_e(c - 1)
-            if two:
-                row_max(tiles[1])
-                exponent(tiles[1])
-                row_sum(done[1])
-            if c == 1:
-                regroup_w(2, 1, nc.vector.tensor_copy)
-            if c == 2:
-                quantise_w(2)
-            if c == N_SLABS - 1:
-                quantise_e(c)
-            for t in done:
-                inverse(t)
-            for t in done:
-                scale_and_store(t)
-            if c == 1:
-                regroup_w(2, 0, nc.scalar.copy)
-
-            ahead = 3 if c < 5 else 4
-            while transposed < min(N_SLABS, c + ahead + 1):
-                transpose_slab(transposed)
-                transposed += 1
-            for t in row_tiles_of(c + 1):
+            if c < 1:
+                while transposed < min(N_SLABS, c + AHEAD + 1):
+                    transpose_x(transposed)
+                    transposed += 1
+            transpose_e(c)
+            for t in tiles[1:]:
+                scores(t)
+            if len(tiles) < 2:
+                for t in tiles:
+                    bank_max(t, 0)
+                    bank_max(t, 1)
+                quantise_x(c + 2)
+                for t in tiles:
+                    row_max(t)
+                    exponent(t)
+                    if t > 0:
+                        row_sum(t - 1)
+                if c >= 5:
+                    quantise_e(c - 1)
+                for t in tiles:
+                    if t > 0:
+                        inverse(t - 1)
+                        scale_and_store(t - 1)
+                if c == 2:
+                    quantise_w(2)
+            else:
+                t = tiles[0]
+                bank_max(t, 0)
+                bank_max(t, 1)
+                quantise_e(c - 1)
+                row_max(t)
+                exponent(t)
+                if c == N_SLABS - 1:
+                    scores(12)
+                bank_max(t + 1, 0)
+                row_sum(t - 1)
+                bank_max(t + 1, 1)
+                inverse(t - 1)
+                if c == N_SLABS - 1:
+                    quantise_e(c)
+                row_max(t + 1)
+                exponent(t + 1)
+                scale_and_store(t - 1)
+                if c == N_SLABS - 1:
+                    row_sum(t - 2)
+                    inverse(t - 2)
+                    scale_and_store(t - 2)
+            for t in row_tiles_of(c + 1)[:1]:
                 scores(t)
 
-        scores(14)
-        scores(15)
+        for t in range(13, 16):
+            scores(t)
         bank_max(12, 0)
         bank_max(12, 1)
-        row_sum(11)
+        row_sum(10)
         row_max(12)
         exponent(12)
-        inverse(11)
-        scale_and_store(11)
+        inverse(10)
+        scale_and_store(10)
         bank_max(13, 0)
         bank_max(13, 1)
-        for t in (14, 15):
-            bank_max(t, 0)
-            row_max(t - 1)
-            exponent(t - 1)
-            bank_max(t, 1)
-            row_sum(t - 2)
+        row_sum(11)
+        row_max(13)
+        exponent(13)
+        inverse(11)
+        scale_and_store(11)
+        bank_max(14, 0)
+        bank_max(14, 1)
+        row_sum(12)
+        row_max(14)
+        exponent(14)
+        inverse(12)
+        bank_max(15, 0)
+        bank_max(15, 1)
+        scale_and_store(12)
         row_max(15)
         exponent(15)
-        for t in (12, 13):
-            inverse(t)
-        for t in (12, 13):
-            scale_and_store(t)
-        for t in (14, 15):
+        for t in (13, 14, 15):
             row_sum(t)
             inverse(t)
             scale_and_store(t)

@@ -21,9 +21,10 @@ N_ROW_TILES = B * T // P
 FLOPS = 2 * (2 * B * T * E * E) + 2 * B * T * T * E
 
 W1_SPLIT = 320
-W2_SPLIT = 320
-VECTOR_SCALES_FROM = 12
+W2_SPLIT = 256
+VECTOR_SCALES_FROM = 13
 AHEAD = 3
+LAST_SPLIT = 640
 
 
 def tile_attentionmm_pa_kernel(tc, x1, x2, W1, W2, b1, b2, out):
@@ -219,7 +220,9 @@ def tile_attentionmm_pa_kernel(tc, x1, x2, W1, W2, b1, b2, out):
 
         def exponent(t):
             ex[t] = expool.tile([P, T], F32, name="ex", tag="ex")
-            sums[t] = small.tile([P, 2], F32, name="sums", tag="sums")
+            g, i = group_of(t)
+            if i == 0:
+                sums[g] = small.tile([P, 2, 2], F32, name="sums", tag="sums")
             for hh in range(2):
                 nc.scalar.activation(
                     out=ex[t][:, BANK * hh : BANK * hh + BANK],
@@ -227,16 +230,21 @@ def tile_attentionmm_pa_kernel(tc, x1, x2, W1, W2, b1, b2, out):
                     func=ACT.Exp,
                     bias=negm[t][:, 0:1],
                     scale=1.0,
-                    accum_out=sums[t][:, hh : hh + 1],
+                    accum_out=sums[g][:, i, hh : hh + 1],
                 )
 
-        def row_sum(t):
-            tot[t] = small.tile([P, 1], F32, name="tot", tag="tot")
-            nc.vector.tensor_reduce(out=tot[t][:], in_=sums[t][:], axis=AX.X, op=ALU.add)
+        def group_of(t):
+            return (t // 2, t % 2) if t < 8 else (t, 0)
+
+        def row_sums(g):
+            n = 2 if g < 4 else 1
+            tot[g] = small.tile([P, 2], F32, name="tot", tag="tot")
+            nc.vector.tensor_reduce(out=tot[g][:, 0:n], in_=sums[g][:, 0:n, :], axis=AX.X, op=ALU.add)
 
         def inverse(t):
+            g, i = group_of(t)
             rs[t] = small.tile([P, 1], F32, name="rs", tag="rs")
-            nc.vector.reciprocal(out=rs[t][:], in_=tot[t][:])
+            nc.vector.reciprocal(out=rs[t][:], in_=tot[g][:, i : i + 1])
 
         def scale_and_store(t):
             if t >= VECTOR_SCALES_FROM:
@@ -246,6 +254,12 @@ def tile_attentionmm_pa_kernel(tc, x1, x2, W1, W2, b1, b2, out):
                     out=ex[t][:], in0=ex[t][:], scalar1=rs[t][:, 0:1], scalar2=0.0, op0=ALU.mult, op1=ALU.add
                 )
             nc.sync.dma_start(out=out_view[:, t // 8, t % 8, :], in_=ex[t][:])
+
+        def scale_and_store_last(t):
+            nc.scalar.activation(out=ex[t][:, LAST_SPLIT:], in_=ex[t][:, LAST_SPLIT:], func=ACT.Copy, scale=rs[t][:, 0:1])
+            nc.vector.tensor_scalar_mul(out=ex[t][:, :LAST_SPLIT], in0=ex[t][:, :LAST_SPLIT], scalar1=rs[t][:, 0:1])
+            nc.sync.dma_start(out=out_view[:, t // 8, t % 8, :LAST_SPLIT], in_=ex[t][:, :LAST_SPLIT])
+            nc.sync.dma_start(out=out_view[:, t // 8, t % 8, LAST_SPLIT:], in_=ex[t][:, LAST_SPLIT:])
 
         def row_tiles_of(c):
             if c < 6:
@@ -293,17 +307,18 @@ def tile_attentionmm_pa_kernel(tc, x1, x2, W1, W2, b1, b2, out):
                     bank_max(t, 0)
                     bank_max(t, 1)
                 quantise_x(c + 2)
+                finish = [t // 2 - 1 for t in tiles if t % 2 == 0 and t > 0]
                 for t in tiles:
                     row_max(t)
                     exponent(t)
-                    if t > 0:
-                        row_sum(t - 1)
+                for g in finish:
+                    row_sums(g)
                 if c >= 5:
                     quantise_e(c - 1)
                 for t in tiles:
-                    if t > 0:
-                        inverse(t - 1)
-                        scale_and_store(t - 1)
+                    if t > 1:
+                        inverse(t - 2)
+                        scale_and_store(t - 2)
                 if c == 2:
                     quantise_w(2)
             else:
@@ -316,18 +331,25 @@ def tile_attentionmm_pa_kernel(tc, x1, x2, W1, W2, b1, b2, out):
                 if c == N_SLABS - 1:
                     scores(12)
                 bank_max(t + 1, 0)
-                row_sum(t - 1)
-                bank_max(t + 1, 1)
-                inverse(t - 1)
                 if c == N_SLABS - 1:
+                    row_sums(8)
+                else:
+                    row_sums(3)
+                bank_max(t + 1, 1)
+                if c == N_SLABS - 1:
+                    inverse(8)
+                    scale_and_store(8)
+                    row_sums(9)
                     quantise_e(c)
+                    inverse(9)
+                    scale_and_store(9)
+                else:
+                    inverse(6)
+                    scale_and_store(6)
+                    inverse(7)
+                    scale_and_store(7)
                 row_max(t + 1)
                 exponent(t + 1)
-                scale_and_store(t - 1)
-                if c == N_SLABS - 1:
-                    row_sum(t - 2)
-                    inverse(t - 2)
-                    scale_and_store(t - 2)
             for t in row_tiles_of(c + 1)[:1]:
                 scores(t)
 
@@ -335,30 +357,35 @@ def tile_attentionmm_pa_kernel(tc, x1, x2, W1, W2, b1, b2, out):
             scores(t)
         bank_max(12, 0)
         bank_max(12, 1)
-        row_sum(10)
+        row_sums(10)
         row_max(12)
         exponent(12)
         inverse(10)
         scale_and_store(10)
         bank_max(13, 0)
         bank_max(13, 1)
-        row_sum(11)
+        row_sums(11)
         row_max(13)
         exponent(13)
         inverse(11)
         scale_and_store(11)
         bank_max(14, 0)
         bank_max(14, 1)
-        row_sum(12)
+        row_sums(12)
         row_max(14)
         exponent(14)
         inverse(12)
         bank_max(15, 0)
-        bank_max(15, 1)
         scale_and_store(12)
+        bank_max(15, 1)
+        row_sums(13)
         row_max(15)
         exponent(15)
-        for t in (13, 14, 15):
-            row_sum(t)
-            inverse(t)
-            scale_and_store(t)
+        inverse(13)
+        scale_and_store(13)
+        row_sums(14)
+        inverse(14)
+        scale_and_store(14)
+        row_sums(15)
+        inverse(15)
+        scale_and_store_last(15)

@@ -20,10 +20,13 @@ N_SLABS = 2 * B * T // SLAB
 N_ROW_TILES = B * T // P
 FLOPS = 2 * (2 * B * T * E * E) + 2 * B * T * T * E
 
-W1_SPLIT = 320
-W2_SPLIT = 256
+W1_SPLIT = 400
+W2_SPLIT = 512
+W2_VECTOR = 1
+W2_SCALAR = -1
 VECTOR_SCALES_FROM = 13
 AHEAD = 3
+X_IN_SCORES = 7
 LAST_SPLIT = 640
 
 
@@ -62,8 +65,11 @@ def tile_attentionmm_pa_kernel(tc, x1, x2, W1, W2, b1, b2, out):
             e_codes[s] = keep.tile([P, B * T], U32, name="e_codes%d" % s, align_bytes=64)
             e_scales[s] = keep.tile([P, B * T], U8, name="e_scales%d" % s, align_bytes=64)
 
-        def load_w(s):
-            nc.sync.dma_start(out=w_sb[s][:], in_=ws[s].rearrange("(q j) c -> q j c", j=4))
+        def load_w(s, c0, c1):
+            nc.sync.dma_start(out=w_sb[s][:, :, c0:c1], in_=ws[s].rearrange("(q j) c -> q j c", j=4)[:, :, c0:c1])
+
+        def load_x_tile(s, b, q, a):
+            nc.sync.dma_start(out=x_sb[s][:, b, q, a, :], in_=x_view[s][:, b, q, a, :])
 
         def load_x(s, b, q0, q1):
             nc.sync.dma_start(out=x_sb[s][:, b, q0:q1, :, :], in_=x_view[s][:, b, q0:q1, :, :])
@@ -71,14 +77,17 @@ def tile_attentionmm_pa_kernel(tc, x1, x2, W1, W2, b1, b2, out):
         def load_b(s, q0, q1):
             nc.sync.dma_start(out=b_sb[s][:, q0:q1, :, :], in_=b_view[s][:, q0:q1, :, :])
 
-        load_x(1, 0, 0, 1)
-        load_w(1)
-        load_x(1, 0, 1, 2)
+        load_x_tile(1, 0, 0, 0)
+        load_w(1, 0, 256)
+        load_w(1, 256, 512)
+        load_x_tile(1, 0, 0, 1)
         load_b(1, 0, 1)
-        load_w(2)
+        load_x(1, 0, 1, 2)
         load_x(1, 0, 2, 3)
+        load_b(1, 1, 2)
         load_x(1, 0, 3, 4)
-        load_b(1, 1, 4)
+        load_w(2, 0, E)
+        load_b(1, 2, 4)
         for half in range(2):
             load_x(2, 0, 2 * half, 2 * half + 2)
             load_b(2, 2 * half, 2 * half + 2)
@@ -97,21 +106,35 @@ def tile_attentionmm_pa_kernel(tc, x1, x2, W1, W2, b1, b2, out):
         def regroup_w(s, c0, c1, copy):
             copy(out=wg[s][:, c0:c1, :], in_=w_sb[s][:, :, c0:c1].rearrange("q j c -> q c j"))
 
-        def quantise_w(s):
+        def quantise_w(s, c0=0, c1=E):
             nc.vector.quantize_mx(
-                out=w_codes[s][:].bitcast(FP8X4),
-                scales=w_scales[s][:],
-                in_=wg[s][:].rearrange("q f j -> q (f j)"),
+                out=w_codes[s][:, c0:c1].bitcast(FP8X4),
+                scales=w_scales[s][:, c0:c1],
+                in_=wg[s][:, c0:c1, :].rearrange("q f j -> q (f j)"),
             )
 
         def first_column(h):
             s, b, q = slabs[h]
             return b * T + q * SLAB
 
+        def transpose_x_tile(a):
+            if a == 0:
+                xg[0] = work.tile([P, SLAB, 4], BF16, name="xg", tag="xg", align_bytes=64)
+            bank = psum.tile([P, BANK], F32, name="tx", tag="tp")
+            words = x_sb[1][:, 0, 0, a, :].bitcast(F32)
+            for u in range(2):
+                nc.tensor.transpose(bank[:, P * u : P * u + P], words[:, u : 256 : 2], ident[:])
+            flat = xg[0][:, P * a : P * a + P, :].rearrange("p m j -> p (m j)").bitcast(F32)
+            nc.scalar.copy(
+                out=flat.rearrange("p (m u) -> p m u", u=2),
+                in_=bank[:, 0:256].rearrange("p (u m) -> p m u", u=2),
+            )
+
         def transpose_x(h):
             s, b, q = slabs[h]
             xg[h] = work.tile([P, SLAB, 4], BF16, name="xg", tag="xg", align_bytes=64)
-            bank = psum.tile([P, BANK], F32, name="tx", tag="tx", bufs=1)
+            tag, n = ("sc", 4) if 1 <= h <= X_IN_SCORES else ("tp", 2)
+            bank = psum.tile([P, BANK], F32, name="tx", tag=tag, bufs=n)
             planes = bank[:].rearrange("p (u a t) -> p u a t", u=2, a=2)
             for a in range(2):
                 words = x_sb[s][:, b, q, a, :].bitcast(F32)
@@ -122,15 +145,15 @@ def tile_attentionmm_pa_kernel(tc, x1, x2, W1, W2, b1, b2, out):
                 in_=bank[:].rearrange("p (u m) -> p m u", u=2),
             )
 
-        def quantise_x(h):
+        def quantise_x(h, m0=0, m1=SLAB):
             if h >= N_SLABS:
                 return
             s = slabs[h][0]
             c0 = first_column(h)
             nc.vector.quantize_mx(
-                out=x_codes[s][:, c0 : c0 + SLAB].bitcast(FP8X4),
-                scales=x_scales[s][:, c0 : c0 + SLAB],
-                in_=xg[h][:].rearrange("p m j -> p (m j)"),
+                out=x_codes[s][:, c0 + m0 : c0 + m1].bitcast(FP8X4),
+                scales=x_scales[s][:, c0 + m0 : c0 + m1],
+                in_=xg[h][:, m0:m1, :].rearrange("p m j -> p (m j)"),
             )
 
         def project(h, a):
@@ -163,7 +186,7 @@ def tile_attentionmm_pa_kernel(tc, x1, x2, W1, W2, b1, b2, out):
         def transpose_e(h):
             s = slabs[h][0]
             eg[h] = work.tile([P, SLAB, 4], BF16, name="eg", tag="eg", align_bytes=64)
-            bank = psum.tile([P, BANK], F32, name="te", tag="te", bufs=1)
+            bank = psum.tile([P, BANK], F32, name="te", tag="tp")
             if s == 1:
                 planes = bank[:].rearrange("p (a u t) -> p u a t", u=2, a=2)
                 src = bank[:].bitcast(BF16).rearrange("p (k t e) -> p t k e", k=4, e=2)
@@ -194,7 +217,7 @@ def tile_attentionmm_pa_kernel(tc, x1, x2, W1, W2, b1, b2, out):
                 if t == N_ROW_TILES - 4:
                     tag, n = "s1", 2
                 elif t == N_ROW_TILES - 3:
-                    tag, n = ("tx", "te")[hh], 1
+                    tag, n = "tp", 2
                 else:
                     tag, n = "sc", 4
                 sc[t, hh] = psum.tile([P, BANK], F32, name="sc", tag=tag, bufs=n)
@@ -268,16 +291,18 @@ def tile_attentionmm_pa_kernel(tc, x1, x2, W1, W2, b1, b2, out):
                 return [c - 6]
             return [2 * c - 20, 2 * c - 19]
 
-        transpose_x(0)
-        regroup_w(1, 0, W1_SPLIT, nc.vector.tensor_copy)
+        transpose_x_tile(0)
+        quantise_x(0, 0, P)
+        regroup_w(1, 0, 256, nc.vector.tensor_copy)
         regroup_w(1, W1_SPLIT, E, nc.scalar.copy)
-        quantise_x(0)
-        quantise_w(1)
+        transpose_x_tile(1)
+        regroup_w(1, 256, W1_SPLIT, nc.vector.tensor_copy)
+        quantise_w(1, 0, 256)
+        quantise_w(1, 256, E)
         transpose_x(1)
         project(0, 0)
+        quantise_x(0, P, SLAB)
         project(0, 1)
-        regroup_w(2, 0, W2_SPLIT, nc.vector.tensor_copy)
-        regroup_w(2, W2_SPLIT, E, nc.scalar.copy)
         transpose_x(2)
         transposed = 3
 
@@ -299,7 +324,11 @@ def tile_attentionmm_pa_kernel(tc, x1, x2, W1, W2, b1, b2, out):
                 while transposed < min(N_SLABS, c + AHEAD + 1):
                     transpose_x(transposed)
                     transposed += 1
+            if c == W2_VECTOR:
+                regroup_w(2, 0, W2_SPLIT, nc.vector.tensor_copy)
             transpose_e(c)
+            if c == W2_SCALAR:
+                regroup_w(2, W2_SPLIT, E, nc.scalar.copy)
             for t in tiles[1:]:
                 scores(t)
             if len(tiles) < 2:

@@ -21,9 +21,9 @@ N_ROW_TILES = B * T // P
 FLOPS = 2 * (2 * B * T * E * E) + 2 * B * T * T * E
 
 W1_SPLIT = 400
-W2_SPLIT = 512
+W2_SPLIT = 256
 W2_VECTOR = 1
-W2_SCALAR = -1
+W2_SCALAR = 0
 VECTOR_SCALES_FROM = 13
 AHEAD = 3
 X_IN_SCORES = 7
@@ -81,16 +81,17 @@ def tile_attentionmm_pa_kernel(tc, x1, x2, W1, W2, b1, b2, out):
         load_w(1, 0, 256)
         load_w(1, 256, 512)
         load_x_tile(1, 0, 0, 1)
-        load_b(1, 0, 1)
         load_x(1, 0, 1, 2)
+        load_b(1, 0, 1)
         load_x(1, 0, 2, 3)
-        load_b(1, 1, 2)
         load_x(1, 0, 3, 4)
+        load_b(1, 1, 2)
+        load_x(2, 0, 0, 2)
         load_w(2, 0, E)
         load_b(1, 2, 4)
-        for half in range(2):
-            load_x(2, 0, 2 * half, 2 * half + 2)
-            load_b(2, 2 * half, 2 * half + 2)
+        load_x(2, 0, 2, 4)
+        load_b(2, 0, 2)
+        load_b(2, 2, 4)
         load_x(1, 1, 0, 4)
         load_x(2, 1, 0, 4)
 
@@ -292,8 +293,8 @@ def tile_attentionmm_pa_kernel(tc, x1, x2, W1, W2, b1, b2, out):
             return [2 * c - 20, 2 * c - 19]
 
         transpose_x_tile(0)
-        quantise_x(0, 0, P)
         regroup_w(1, 0, 256, nc.vector.tensor_copy)
+        quantise_x(0, 0, P)
         regroup_w(1, W1_SPLIT, E, nc.scalar.copy)
         transpose_x_tile(1)
         regroup_w(1, 256, W1_SPLIT, nc.vector.tensor_copy)
@@ -304,7 +305,8 @@ def tile_attentionmm_pa_kernel(tc, x1, x2, W1, W2, b1, b2, out):
         quantise_x(0, P, SLAB)
         project(0, 1)
         transpose_x(2)
-        transposed = 3
+        transpose_x(3)
+        transposed = 4
 
         for c in range(N_SLABS):
             tiles = row_tiles_of(c)
@@ -385,32 +387,32 @@ def tile_attentionmm_pa_kernel(tc, x1, x2, W1, W2, b1, b2, out):
         for t in range(13, 16):
             scores(t)
         bank_max(12, 0)
-        bank_max(12, 1)
         row_sums(10)
-        row_max(12)
-        exponent(12)
+        bank_max(12, 1)
         inverse(10)
         scale_and_store(10)
+        row_max(12)
+        exponent(12)
         bank_max(13, 0)
-        bank_max(13, 1)
         row_sums(11)
-        row_max(13)
-        exponent(13)
+        bank_max(13, 1)
         inverse(11)
         scale_and_store(11)
+        row_max(13)
+        exponent(13)
         bank_max(14, 0)
-        bank_max(14, 1)
         row_sums(12)
+        bank_max(14, 1)
+        inverse(12)
+        scale_and_store(12)
         row_max(14)
         exponent(14)
-        inverse(12)
         bank_max(15, 0)
-        scale_and_store(12)
-        bank_max(15, 1)
         row_sums(13)
+        bank_max(15, 1)
+        inverse(13)
         row_max(15)
         exponent(15)
-        inverse(13)
         scale_and_store(13)
         row_sums(14)
         inverse(14)

@@ -288,9 +288,7 @@ def tile_attentionmm_pa_kernel(tc, x1, x2, W1, W2, b1, b2, out):
         def row_tiles_of(c):
             if c < 6:
                 return []
-            if c < 14:
-                return [c - 6]
-            return [2 * c - 20, 2 * c - 19]
+            return [c - 6]
 
         transpose_x_tile(0)
         regroup_w(1, 0, 256, nc.vector.tensor_copy)
@@ -308,7 +306,7 @@ def tile_attentionmm_pa_kernel(tc, x1, x2, W1, W2, b1, b2, out):
         transpose_x(3)
         transposed = 4
 
-        for c in range(N_SLABS):
+        for c in range(N_SLABS - 2):
             tiles = row_tiles_of(c)
             if c >= 1:
                 while transposed < min(N_SLABS, c + AHEAD + 1):
@@ -331,58 +329,69 @@ def tile_attentionmm_pa_kernel(tc, x1, x2, W1, W2, b1, b2, out):
             transpose_e(c)
             if c == W2_SCALAR:
                 regroup_w(2, W2_SPLIT, E, nc.scalar.copy)
-            for t in tiles[1:]:
-                scores(t)
-            if len(tiles) < 2:
-                for t in tiles:
-                    bank_max(t, 0)
-                    bank_max(t, 1)
-                quantise_x(c + 2)
-                finish = [t // 2 - 1 for t in tiles if t % 2 == 0 and t > 0]
-                for t in tiles:
-                    row_max(t)
-                    exponent(t)
-                for g in finish:
-                    row_sums(g)
-                if c >= 5:
-                    quantise_e(c - 1)
-                for t in tiles:
-                    if t > 1:
-                        inverse(t - 2)
-                        scale_and_store(t - 2)
-                if c == 2:
-                    quantise_w(2)
-            else:
-                t = tiles[0]
+            for t in tiles:
                 bank_max(t, 0)
                 bank_max(t, 1)
-                quantise_e(c - 1)
+            quantise_x(c + 2)
+            finish = [t // 2 - 1 for t in tiles if t % 2 == 0 and t > 0]
+            for t in tiles:
                 row_max(t)
                 exponent(t)
-                if c == N_SLABS - 1:
-                    scores(12)
-                bank_max(t + 1, 0)
-                if c == N_SLABS - 1:
-                    row_sums(8)
-                else:
-                    row_sums(3)
-                bank_max(t + 1, 1)
-                if c == N_SLABS - 1:
-                    inverse(8)
-                    scale_and_store(8)
-                    row_sums(9)
-                    quantise_e(c)
-                    inverse(9)
-                    scale_and_store(9)
-                else:
-                    inverse(6)
-                    scale_and_store(6)
-                    inverse(7)
-                    scale_and_store(7)
-                row_max(t + 1)
-                exponent(t + 1)
-            for t in row_tiles_of(c + 1)[:1]:
+            for g in finish:
+                row_sums(g)
+            if c >= 5:
+                quantise_e(c - 1)
+            for t in tiles:
+                if t > 1:
+                    inverse(t - 2)
+                    scale_and_store(t - 2)
+            if c == 2:
+                quantise_w(2)
+            for t in row_tiles_of(c + 1):
                 scores(t)
+
+        add_bias(14, 0)
+        project(15, 0)
+        add_bias(14, 1)
+        project(15, 1)
+        transpose_e(14)
+        scores(9)
+        bank_max(8, 0)
+        row_sums(3)
+        bank_max(8, 1)
+        quantise_e(13)
+        inverse(6)
+        scale_and_store(6)
+        row_max(8)
+        exponent(8)
+        bank_max(9, 0)
+        bank_max(9, 1)
+        inverse(7)
+        scale_and_store(7)
+        scores(10)
+        add_bias(15, 0)
+        row_max(9)
+        exponent(9)
+        add_bias(15, 1)
+        transpose_e(15)
+        scores(11)
+        bank_max(10, 0)
+        row_sums(8)
+        bank_max(10, 1)
+        quantise_e(14)
+        inverse(8)
+        scale_and_store(8)
+        row_max(10)
+        exponent(10)
+        scores(12)
+        bank_max(11, 0)
+        row_sums(9)
+        bank_max(11, 1)
+        quantise_e(15)
+        inverse(9)
+        scale_and_store(9)
+        row_max(11)
+        exponent(11)
 
         for t in range(13, 16):
             scores(t)

@@ -26,6 +26,7 @@ W2_VECTOR = 1
 W2_SCALAR = 0
 VECTOR_SCALES_FROM = 13
 AHEAD = 3
+W_HALF = 256
 X_IN_SCORES = 7
 LAST_SPLIT = 640
 
@@ -163,15 +164,17 @@ def tile_attentionmm_pa_kernel(tc, x1, x2, W1, W2, b1, b2, out):
             s = slabs[h][0]
             c0 = first_column(h) + P * a
             s1[h, a] = psum.tile([P, BANK], F32, name="s1", tag="s1")
-            nc.tensor.matmul_mx(
-                out=s1[h, a][:],
-                lhsT=x_codes[s][:, c0 : c0 + P].bitcast(FP8X4),
-                lhsT_scale=x_scales[s][:, c0 : c0 + P],
-                rhs=w_codes[s][:].bitcast(FP8X4),
-                rhs_scale=w_scales[s][:],
-                start=True,
-                stop=True,
-            )
+            cuts = (0, W_HALF, E) if (h, a) == (0, 0) else (0, E)
+            for f0, f1 in zip(cuts, cuts[1:]):
+                nc.tensor.matmul_mx(
+                    out=s1[h, a][:, f0:f1],
+                    lhsT=x_codes[s][:, c0 : c0 + P].bitcast(FP8X4),
+                    lhsT_scale=x_scales[s][:, c0 : c0 + P],
+                    rhs=w_codes[s][:, f0:f1].bitcast(FP8X4),
+                    rhs_scale=w_scales[s][:, f0:f1],
+                    start=True,
+                    stop=True,
+                )
 
         def add_bias(h, a):
             s, b, q = slabs[h]
@@ -308,7 +311,7 @@ def tile_attentionmm_pa_kernel(tc, x1, x2, W1, W2, b1, b2, out):
 
         for c in range(N_SLABS - 2):
             tiles = row_tiles_of(c)
-            if c >= 1:
+            if 1 <= c < 6:
                 while transposed < min(N_SLABS, c + AHEAD + 1):
                     transpose_x(transposed)
                     transposed += 1
@@ -317,9 +320,9 @@ def tile_attentionmm_pa_kernel(tc, x1, x2, W1, W2, b1, b2, out):
                 quantise_x(1)
             if c <= 5:
                 quantise_e(c - 2)
-            project(c + 1, 0)
+            if c < 6:
+                project(c + 1, 0)
             add_bias(c, 1)
-            project(c + 1, 1)
             if c < 1:
                 while transposed < min(N_SLABS, c + AHEAD + 1):
                     transpose_x(transposed)
@@ -327,6 +330,13 @@ def tile_attentionmm_pa_kernel(tc, x1, x2, W1, W2, b1, b2, out):
             if c == W2_VECTOR:
                 regroup_w(2, 0, W2_SPLIT, nc.vector.tensor_copy)
             transpose_e(c)
+            if c >= 6:
+                while transposed < min(N_SLABS, c + AHEAD + 1):
+                    transpose_x(transposed)
+                    transposed += 1
+            if c >= 6:
+                project(c + 1, 0)
+            project(c + 1, 1)
             if c == W2_SCALAR:
                 regroup_w(2, W2_SPLIT, E, nc.scalar.copy)
             for t in tiles:
@@ -351,10 +361,10 @@ def tile_attentionmm_pa_kernel(tc, x1, x2, W1, W2, b1, b2, out):
                 scores(t)
 
         add_bias(14, 0)
-        project(15, 0)
         add_bias(14, 1)
-        project(15, 1)
         transpose_e(14)
+        project(15, 0)
+        project(15, 1)
         scores(9)
         bank_max(8, 0)
         row_sums(3)

from contextlib import ExitStack

import concourse.mybir as mybir
from concourse.masks import make_identity

F32 = mybir.dt.float32
BF16 = mybir.dt.bfloat16
U32 = mybir.dt.uint32
U8 = mybir.dt.uint8
FP8X4 = mybir.dt.float8_e4m3fn_x4
ALU = mybir.AluOpType
ACT = mybir.ActivationFunctionType
AX = mybir.AxisListType

B, T, E = 2, 1024, 512
P = 128
BANK = 512
SLAB = 256
N_SLABS = 2 * B * T // SLAB
N_ROW_TILES = B * T // P
FLOPS = 2 * (2 * B * T * E * E) + 2 * B * T * T * E

W1_SPLIT = 400
W2_SPLIT = 256
W2_VECTOR = 1
W2_SCALAR = 0
VECTOR_SCALES_FROM = 13
AHEAD = 3
W_HALF = 256
X_IN_SCORES = 7
LAST_SPLIT = 640


def tile_attentionmm_pa_kernel(tc, x1, x2, W1, W2, b1, b2, out):
    nc = tc.nc
    with ExitStack() as ctx:
        ctx.enter_context(tc.manual_schedule())
        keep = ctx.enter_context(tc.tile_pool(name="keep", bufs=1))
        work = ctx.enter_context(tc.tile_pool(name="work", bufs=6))
        expool = ctx.enter_context(tc.tile_pool(name="expool", bufs=8))
        small = ctx.enter_context(tc.tile_pool(name="small", bufs=8))
        psum = ctx.enter_context(tc.psum_pool(name="psum", bufs=2))

        ws = {1: W1, 2: W2}
        x_view = {
            1: x1.rearrange("b (q p a) k -> p b q a k", q=4, a=2),
            2: x2.rearrange("b (p q a) k -> p b q a k", q=4, a=2),
        }
        b_view = {
            1: b1.rearrange("(q p a) f -> p q a f", q=4, a=2),
            2: b2.rearrange("(p q a) f -> p q a f", q=4, a=2),
        }
        out_view = out.rearrange("b (p n) j -> p b n j", p=P)

        x_sb, b_sb, w_sb, wg, w_codes, w_scales = {}, {}, {}, {}, {}, {}
        x_codes, x_scales, e_codes, e_scales = {}, {}, {}, {}
        for s in (1, 2):
            x_sb[s] = keep.tile([P, B, 4, 2, E], BF16, name="x_sb%d" % s)
            b_sb[s] = keep.tile([P, 4, 2, E], BF16, name="b_sb%d" % s)
            w_sb[s] = keep.tile([P, 4, E], BF16, name="w_sb%d" % s)
            wg[s] = keep.tile([P, E, 4], BF16, name="wg%d" % s, align_bytes=64)
            w_codes[s] = keep.tile([P, E], U32, name="w_codes%d" % s, align_bytes=64)
            w_scales[s] = keep.tile([P, E], U8, name="w_scales%d" % s, align_bytes=64)
            x_codes[s] = keep.tile([P, B * T], U32, name="x_codes%d" % s, align_bytes=64)
            x_scales[s] = keep.tile([P, B * T], U8, name="x_scales%d" % s, align_bytes=64)
            e_codes[s] = keep.tile([P, B * T], U32, name="e_codes%d" % s, align_bytes=64)
            e_scales[s] = keep.tile([P, B * T], U8, name="e_scales%d" % s, align_bytes=64)

        def load_w(s, c0, c1):
            nc.sync.dma_start(out=w_sb[s][:, :, c0:c1], in_=ws[s].rearrange("(q j) c -> q j c", j=4)[:, :, c0:c1])

        def load_x_tile(s, b, q, a):
            nc.sync.dma_start(out=x_sb[s][:, b, q, a, :], in_=x_view[s][:, b, q, a, :])

        def load_x(s, b, q0, q1):
            nc.sync.dma_start(out=x_sb[s][:, b, q0:q1, :, :], in_=x_view[s][:, b, q0:q1, :, :])

        def load_b(s, q0, q1):
            nc.sync.dma_start(out=b_sb[s][:, q0:q1, :, :], in_=b_view[s][:, q0:q1, :, :])

        load_x_tile(1, 0, 0, 0)
        load_w(1, 0, 256)
        load_w(1, 256, 512)
        load_x_tile(1, 0, 0, 1)
        load_x(1, 0, 1, 2)
        load_b(1, 0, 1)
        load_x(1, 0, 2, 3)
        load_x(1, 0, 3, 4)
        load_b(1, 1, 2)
        load_x(2, 0, 0, 2)
        load_w(2, 0, E)
        load_b(1, 2, 4)
        load_x(2, 0, 2, 4)
        load_b(2, 0, 2)
        load_b(2, 2, 4)
        load_x(1, 1, 0, 4)
        load_x(2, 1, 0, 4)

        ident = keep.tile([P, P], F32, name="ident")
        make_identity(nc, ident[:])
        warm = keep.tile([P, 1], F32, name="warm")
        nc.vector.memset(warm[:], 0.0)
        nc.scalar.activation(out=warm[:], in_=warm[:], func=ACT.Exp)

        slabs = [(s, b, q) for b in range(B) for s in (1, 2) for q in range(4)]
        xg, pre, eg, s1, sc, part, negm, ex, sums, tot, rs = {}, {}, {}, {}, {}, {}, {}, {}, {}, {}, {}

        def regroup_w(s, c0, c1, copy):
            copy(out=wg[s][:, c0:c1, :], in_=w_sb[s][:, :, c0:c1].rearrange("q j c -> q c j"))

        def quantise_w(s, c0=0, c1=E):
            nc.vector.quantize_mx(
                out=w_codes[s][:, c0:c1].bitcast(FP8X4),
                scales=w_scales[s][:, c0:c1],
                in_=wg[s][:, c0:c1, :].rearrange("q f j -> q (f j)"),
            )

        def first_column(h):
            s, b, q = slabs[h]
            return b * T + q * SLAB

        def transpose_x_tile(a):
            if a == 0:
                xg[0] = work.tile([P, SLAB, 4], BF16, name="xg", tag="xg", align_bytes=64)
            bank = psum.tile([P, BANK], F32, name="tx", tag="tp")
            words = x_sb[1][:, 0, 0, a, :].bitcast(F32)
            for u in range(2):
                nc.tensor.transpose(bank[:, P * u : P * u + P], words[:, u : 256 : 2], ident[:])
            flat = xg[0][:, P * a : P * a + P, :].rearrange("p m j -> p (m j)").bitcast(F32)
            nc.scalar.copy(
                out=flat.rearrange("p (m u) -> p m u", u=2),
                in_=bank[:, 0:256].rearrange("p (u m) -> p m u", u=2),
            )

        def transpose_x(h):
            s, b, q = slabs[h]
            xg[h] = work.tile([P, SLAB, 4], BF16, name="xg", tag="xg", align_bytes=64)
            tag, n = ("sc", 4) if 1 <= h <= X_IN_SCORES else ("tp", 2)
            bank = psum.tile([P, BANK], F32, name="tx", tag=tag, bufs=n)
            planes = bank[:].rearrange("p (u a t) -> p u a t", u=2, a=2)
            for a in range(2):
                words = x_sb[s][:, b, q, a, :].bitcast(F32)
                for u in range(2):
                    nc.tensor.transpose(planes[:, u, a, :], words[:, u : 256 : 2], ident[:])
            nc.scalar.copy(
                out=xg[h][:].rearrange("p m j -> p (m j)").bitcast(F32).rearrange("p (m u) -> p m u", u=2),
                in_=bank[:].rearrange("p (u m) -> p m u", u=2),
            )

        def quantise_x(h, m0=0, m1=SLAB):
            if h >= N_SLABS:
                return
            s = slabs[h][0]
            c0 = first_column(h)
            nc.vector.quantize_mx(
                out=x_codes[s][:, c0 + m0 : c0 + m1].bitcast(FP8X4),
                scales=x_scales[s][:, c0 + m0 : c0 + m1],
                in_=xg[h][:, m0:m1, :].rearrange("p m j -> p (m j)"),
            )

        def project(h, a):
            if h >= N_SLABS:
                return
            s = slabs[h][0]
            c0 = first_column(h) + P * a
            s1[h, a] = psum.tile([P, BANK], F32, name="s1", tag="s1")
            cuts = (0, W_HALF, E) if (h, a) == (0, 0) else (0, E)
            for f0, f1 in zip(cuts, cuts[1:]):
                nc.tensor.matmul_mx(
                    out=s1[h, a][:, f0:f1],
                    lhsT=x_codes[s][:, c0 : c0 + P].bitcast(FP8X4),
                    lhsT_scale=x_scales[s][:, c0 : c0 + P],
                    rhs=w_codes[s][:, f0:f1].bitcast(FP8X4),
                    rhs_scale=w_scales[s][:, f0:f1],
                    start=True,
                    stop=True,
                )

        def add_bias(h, a):
            s, b, q = slabs[h]
            if a == 0:
                pre[h] = work.tile([P, 2, E], BF16, name="pre", tag="pre", align_bytes=64)
            nc.vector.tensor_tensor(
                out=pre[h][:, a, :].rearrange("q (u p e) -> q u p e", u=2, e=2),
                in0=s1[h, a][:].rearrange("q (p u e) -> q u p e", u=2, e=2),
                in1=b_sb[s][:, q, a, :].rearrange("q (p u e) -> q u p e", u=2, e=2),
                op=ALU.add,
            )

        def transpose_e(h):
            s = slabs[h][0]
            eg[h] = work.tile([P, SLAB, 4], BF16, name="eg", tag="eg", align_bytes=64)
            bank = psum.tile([P, BANK], F32, name="te", tag="tp")
            if s == 1:
                planes = bank[:].rearrange("p (a u t) -> p u a t", u=2, a=2)
                src = bank[:].bitcast(BF16).rearrange("p (k t e) -> p t k e", k=4, e=2)
                dst = eg[h][:].rearrange("p (t a) (u e) -> p t (a u) e", a=2, e=2)
            else:
                planes = bank[:].rearrange("p (u a t) -> p u a t", u=2, a=2)
                src = bank[:].bitcast(BF16).rearrange("p (u m e) -> p m u e", u=2, e=2)
                dst = eg[h][:].rearrange("p m (u e) -> p m u e", e=2)
            for a in range(2):
                words = pre[h][:, a, :].bitcast(F32)
                for u in range(2):
                    nc.tensor.transpose(planes[:, u, a, :], words[:, P * u : P * u + P], ident[:])
            nc.scalar.activation(out=dst, in_=src, func=ACT.Relu)

        def quantise_e(h):
            if h < 0:
                return
            s = slabs[h][0]
            c0 = first_column(h)
            nc.vector.quantize_mx(
                out=e_codes[s][:, c0 : c0 + SLAB].bitcast(FP8X4),
                scales=e_scales[s][:, c0 : c0 + SLAB],
                in_=eg[h][:].rearrange("p m j -> p (m j)"),
            )

        def scores(t):
            for hh in range(2):
                if t == N_ROW_TILES - 4:
                    tag, n = "s1", 2
                elif t == N_ROW_TILES - 3:
                    tag, n = "tp", 2
                else:
                    tag, n = "sc", 4
                sc[t, hh] = psum.tile([P, BANK], F32, name="sc", tag=tag, bufs=n)
                j0 = (t // 8) * T + BANK * hh
                nc.tensor.matmul_mx(
                    out=sc[t, hh][:],
                    lhsT=e_codes[2][:, P * t : P * t + P].bitcast(FP8X4),
                    lhsT_scale=e_scales[2][:, P * t : P * t + P],
                    rhs=e_codes[1][:, j0 : j0 + BANK].bitcast(FP8X4),
                    rhs_scale=e_scales[1][:, j0 : j0 + BANK],
                    start=True,
                    stop=True,
                )

        def bank_max(t, hh):
            if hh == 0:
                part[t] = small.tile([P, 2], F32, name="part", tag="part")
            nc.vector.tensor_reduce(out=part[t][:, hh : hh + 1], in_=sc[t, hh][:], axis=AX.X, op=ALU.max)

        def row_max(t):
            negm[t] = small.tile([P, 1], F32, name="negm", tag="negm")
            nc.vector.tensor_reduce(out=negm[t][:], in_=part[t][:], axis=AX.X, op=ALU.max, negate=True)

        def exponent(t):
            ex[t] = expool.tile([P, T], F32, name="ex", tag="ex")
            g, i = group_of(t)
            if i == 0:
                sums[g] = small.tile([P, 2, 2], F32, name="sums", tag="sums")
            for hh in range(2):
                nc.scalar.activation(
                    out=ex[t][:, BANK * hh : BANK * hh + BANK],
                    in_=sc[t, hh][:],
                    func=ACT.Exp,
                    bias=negm[t][:, 0:1],
                    scale=1.0,
                    accum_out=sums[g][:, i, hh : hh + 1],
                )

        def group_of(t):
            return (t // 2, t % 2) if t < 8 else (t, 0)

        def row_sums(g):
            n = 2 if g < 4 else 1
            tot[g] = small.tile([P, 2], F32, name="tot", tag="tot")
            nc.vector.tensor_reduce(out=tot[g][:, 0:n], in_=sums[g][:, 0:n, :], axis=AX.X, op=ALU.add)

        def inverse(t):
            g, i = group_of(t)
            rs[t] = small.tile([P, 1], F32, name="rs", tag="rs")
            nc.vector.reciprocal(out=rs[t][:], in_=tot[g][:, i : i + 1])

        def scale_and_store(t):
            if t >= VECTOR_SCALES_FROM:
                nc.vector.tensor_scalar_mul(out=ex[t][:], in0=ex[t][:], scalar1=rs[t][:, 0:1])
            else:
                nc.gpsimd.tensor_scalar(
                    out=ex[t][:], in0=ex[t][:], scalar1=rs[t][:, 0:1], scalar2=0.0, op0=ALU.mult, op1=ALU.add
                )
            nc.sync.dma_start(out=out_view[:, t // 8, t % 8, :], in_=ex[t][:])

        def scale_and_store_last(t):
            nc.scalar.activation(out=ex[t][:, LAST_SPLIT:], in_=ex[t][:, LAST_SPLIT:], func=ACT.Copy, scale=rs[t][:, 0:1])
            nc.vector.tensor_scalar_mul(out=ex[t][:, :LAST_SPLIT], in0=ex[t][:, :LAST_SPLIT], scalar1=rs[t][:, 0:1])
            nc.sync.dma_start(out=out_view[:, t // 8, t % 8, :LAST_SPLIT], in_=ex[t][:, :LAST_SPLIT])
            nc.sync.dma_start(out=out_view[:, t // 8, t % 8, LAST_SPLIT:], in_=ex[t][:, LAST_SPLIT:])

        def row_tiles_of(c):
            if c < 6:
                return []
            return [c - 6]

        transpose_x_tile(0)
        regroup_w(1, 0, 256, nc.vector.tensor_copy)
        quantise_x(0, 0, P)
        regroup_w(1, W1_SPLIT, E, nc.scalar.copy)
        transpose_x_tile(1)
        regroup_w(1, 256, W1_SPLIT, nc.vector.tensor_copy)
        quantise_w(1, 0, 256)
        quantise_w(1, 256, E)
        transpose_x(1)
        project(0, 0)
        quantise_x(0, P, SLAB)
        project(0, 1)
        transpose_x(2)
        transpose_x(3)
        transposed = 4

        for c in range(N_SLABS - 2):
            tiles = row_tiles_of(c)
            if 1 <= c < 6:
                while transposed < min(N_SLABS, c + AHEAD + 1):
                    transpose_x(transposed)
                    transposed += 1
            add_bias(c, 0)
            if c == 0:
                quantise_x(1)
            if c <= 5:
                quantise_e(c - 2)
            if c < 6:
                project(c + 1, 0)
            add_bias(c, 1)
            if c < 1:
                while transposed < min(N_SLABS, c + AHEAD + 1):
                    transpose_x(transposed)
                    transposed += 1
            if c == W2_VECTOR:
                regroup_w(2, 0, W2_SPLIT, nc.vector.tensor_copy)
            transpose_e(c)
            if c >= 6:
                while transposed < min(N_SLABS, c + AHEAD + 1):
                    transpose_x(transposed)
                    transposed += 1
            if c >= 6:
                project(c + 1, 0)
            project(c + 1, 1)
            if c == W2_SCALAR:
                regroup_w(2, W2_SPLIT, E, nc.scalar.copy)
            for t in tiles:
                bank_max(t, 0)
                bank_max(t, 1)
            quantise_x(c + 2)
            finish = [t // 2 - 1 for t in tiles if t % 2 == 0 and t > 0]
            for t in tiles:
                row_max(t)
                exponent(t)
            for g in finish:
                row_sums(g)
            if c >= 5:
                quantise_e(c - 1)
            for t in tiles:
                if t > 1:
                    inverse(t - 2)
                    scale_and_store(t - 2)
            if c == 2:
                quantise_w(2)
            for t in row_tiles_of(c + 1):
                scores(t)

        add_bias(14, 0)
        add_bias(14, 1)
        transpose_e(14)
        project(15, 0)
        project(15, 1)
        scores(9)
        bank_max(8, 0)
        row_sums(3)
        bank_max(8, 1)
        quantise_e(13)
        inverse(6)
        scale_and_store(6)
        row_max(8)
        exponent(8)
        bank_max(9, 0)
        bank_max(9, 1)
        inverse(7)
        scale_and_store(7)
        scores(10)
        add_bias(15, 0)
        row_max(9)
        exponent(9)
        add_bias(15, 1)
        transpose_e(15)
        scores(11)
        bank_max(10, 0)
        row_sums(8)
        bank_max(10, 1)
        quantise_e(14)
        inverse(8)
        scale_and_store(8)
        row_max(10)
        exponent(10)
        scores(12)
        bank_max(11, 0)
        row_sums(9)
        bank_max(11, 1)
        quantise_e(15)
        inverse(9)
        scale_and_store(9)
        row_max(11)
        exponent(11)

        for t in range(13, 16):
            scores(t)
        bank_max(12, 0)
        row_sums(10)
        bank_max(12, 1)
        inverse(10)
        scale_and_store(10)
        row_max(12)
        exponent(12)
        bank_max(13, 0)
        row_sums(11)
        bank_max(13, 1)
        inverse(11)
        scale_and_store(11)
        row_max(13)
        exponent(13)
        bank_max(14, 0)
        row_sums(12)
        bank_max(14, 1)
        inverse(12)
        scale_and_store(12)
        row_max(14)
        exponent(14)
        bank_max(15, 0)
        row_sums(13)
        bank_max(15, 1)
        inverse(13)
        row_max(15)
        exponent(15)
        scale_and_store(13)
        row_sums(14)
        inverse(14)
        scale_and_store(14)
        row_sums(15)
        inverse(15)
        scale_and_store_last(15)
